import numpy as np
import ml_dtypes


def mxq(x, axis, fmt="e4m3"):
    dtype, down = {"e4m3": (ml_dtypes.float8_e4m3fn, 7), "e5m2": (ml_dtypes.float8_e5m2, 14)}[fmt]
    v = np.moveaxis(np.asarray(x, np.float32).astype(ml_dtypes.bfloat16).astype(np.float64), axis, -1)
    blocks = v.reshape(v.shape[:-1] + (-1, 32))
    amax = np.abs(blocks).max(-1, keepdims=True)
    byte = np.maximum(np.where(amax > 0, np.frexp(amax)[1] - 1 + 127, 0) - down, 1)
    scale = np.exp2(byte - 127.0)
    codes = (blocks / scale).astype(np.float32).astype(dtype).astype(np.float64)
    return np.moveaxis((codes * scale).reshape(v.shape), -1, axis)


WIDE = False


def mx_kscale(k):
    if not WIDE:
        return np.ones(k)
    levels = np.array([10, -10, 5, -5, 0])
    a = np.random.permutation(np.resize(levels, k // 512 * 4)).reshape(k // 512, 4)
    idx = np.arange(k)
    return np.exp2(a[idx // 512, idx % 128 // 32])


BF16 = ml_dtypes.bfloat16


def bf(x):
    return np.asarray(x, np.float32).astype(BF16)


def f64(x):
    return np.asarray(x).astype(np.float64)


N, C, F, H, W, KH, KW = 72, 8192, 64, 4, 4, 3, 3
P = H * W


def setup_inputs():
    s = mx_kscale(C)[None, :, None, None]
    return {"x_dct": bf(np.random.standard_normal((N, C, H, W)) * 2.0 * s),
            "k_dct": bf(np.random.standard_normal((F, C, H, W)) * 2.0 / np.sqrt(C) / s)}


def reference(x_dct, k_dct):
    xq = mxq(f64(x_dct), 1, "e4m3").reshape(N, C, P).transpose(2, 0, 1)
    kq = mxq(f64(k_dct), 1, "e4m3").reshape(F, C, P).transpose(2, 1, 0)
    r = xq @ kq
    return r.transpose(1, 2, 0).reshape(N, F, H, W)

@@ -1,0 +1,140 @@
+from contextlib import ExitStack
+
+import concourse.mybir as mybir
+from concourse.masks import make_identity
+
+BF16 = mybir.dt.bfloat16
+F32 = mybir.dt.float32
+U32 = mybir.dt.uint32
+U8 = mybir.dt.uint8
+FP8X4 = mybir.dt.float8_e4m3fn_x4
+
+P = 128
+PACK = 4
+IMAGES = 72
+FILTERS = 64
+CHANNELS = 8192
+FREQS = 16
+
+SEGMENTS = 64
+QUARTERS = 4
+HALVES = 2
+WORDS = 4
+RUN = WORDS * PACK * FREQS
+
+ROWS = 8
+QUANT_COLS = 1024
+PAIRS = FREQS // 2
+WINDOW = 256
+STEP = 64
+
+FLOPS = 2 * IMAGES * FILTERS * CHANNELS * FREQS
+
+
+def load_and_regroup(nc, raw_pool, copy, source, quarter, rows, grouped):
+    view = source.rearrange(
+        "n (s q i c) h w -> q i s n (c h w)", s=SEGMENTS, q=QUARTERS, i=HALVES
+    )
+    for r0 in range(0, rows, ROWS):
+        raw = raw_pool.tile([P, ROWS, RUN], BF16)
+        for i in range(HALVES):
+            nc.sync.dma_start(out=raw[i:P:HALVES, :, :], in_=view[quarter, i, :, r0 : r0 + ROWS, :])
+        by_word = raw[:].rearrange("p n (j t f) -> p j f n t", j=WORDS, t=PACK)
+        for j in range(WORDS):
+            copy(out=grouped[j][:, :, r0 : r0 + ROWS, :], in_=by_word[:, j])
+
+
+def quantise(nc, grouped, codes, scales, cols):
+    flat = grouped[:].rearrange("p f n t -> p (f n t)")
+    for c0 in range(0, cols, QUANT_COLS):
+        c1 = min(c0 + QUANT_COLS, cols)
+        nc.vector.quantize_mx(
+            out=codes[:, c0:c1].bitcast(FP8X4),
+            scales=scales[:, c0:c1],
+            in_=flat[:, PACK * c0 : PACK * c1],
+        )
+
+
+def tile_convdct_pa_k_kernel(tc, x_dct, k_dct, out):
+    nc = tc.nc
+    x_cols = FREQS * IMAGES
+    k_cols = FREQS * FILTERS
+    with ExitStack() as ctx:
+        consts = ctx.enter_context(tc.tile_pool(name="consts", bufs=1))
+        raw_pool = ctx.enter_context(tc.tile_pool(name="raw", bufs=16))
+        grouped_pool = ctx.enter_context(tc.tile_pool(name="grouped", bufs=5))
+        k_mx = ctx.enter_context(tc.tile_pool(name="k_mx", bufs=6))
+        x_mx = ctx.enter_context(tc.tile_pool(name="x_mx", bufs=2))
+        psum = ctx.enter_context(tc.psum_pool(name="psum", bufs=1))
+
+        identity = consts.tile([P, P], F32)
+        make_identity(nc, identity[:])
+        sums = consts.tile([P, PAIRS, P], F32)
+        nc.vector.memset(sums[:], 0.0)
+
+        acc = [psum.tile([P, WINDOW], F32, name="acc%d" % b) for b in range(PAIRS)]
+
+        for q in range(QUARTERS):
+            k_grouped = [
+                grouped_pool.tile([P, FREQS, FILTERS, PACK], BF16, name="kg%d" % j, tag="kg", align_bytes=64)
+                for j in range(WORDS)
+            ]
+            load_and_regroup(nc, raw_pool, nc.scalar.copy, k_dct, q, FILTERS, k_grouped)
+            k_codes = []
+            k_scales = []
+            for j in range(WORDS):
+                codes = k_mx.tile([P, k_cols], U32, name="kc%d" % j, tag="kc", align_bytes=64)
+                scales = k_mx.tile([P, k_cols], U8, name="ks%d" % j, tag="ks", align_bytes=64)
+                quantise(nc, k_grouped[j], codes, scales, k_cols)
+                k_codes.append(codes)
+                k_scales.append(scales)
+
+            x_grouped = [
+                grouped_pool.tile([P, FREQS, IMAGES, PACK], BF16, name="xg%d" % j, tag="xg", align_bytes=64)
+                for j in range(WORDS)
+            ]
+            load_and_regroup(nc, raw_pool, nc.vector.tensor_copy, x_dct, q, IMAGES, x_grouped)
+            for j in range(WORDS):
+                x_codes = x_mx.tile([P, x_cols], U32, align_bytes=64)
+                x_scales = x_mx.tile([P, x_cols], U8, align_bytes=64)
+                quantise(nc, x_grouped[j], x_codes, x_scales, x_cols)
+                for b in range(PAIRS):
+                    w0 = window_start(b)
+                    nc.tensor.matmul_mx(
+                        out=acc[b][:],
+                        lhsT=k_codes[j][:, P * b : P * (b + 1)].bitcast(FP8X4),
+                        lhsT_scale=k_scales[j][:, P * b : P * (b + 1)],
+                        rhs=x_codes[:, w0 : w0 + WINDOW].bitcast(FP8X4),
+                        rhs_scale=x_scales[:, w0 : w0 + WINDOW],
+                        start=(q == 0 and j == 0),
+                        stop=(q == QUARTERS - 1 and j == WORDS - 1),
+                    )
+
+        for b in range(PAIRS):
+            first = 2 * IMAGES * b - window_start(b)
+            nc.vector.tensor_copy(out=sums[0:FILTERS, b, 0:IMAGES], in_=acc[b][0:FILTERS, first : first + IMAGES])
+            nc.scalar.copy(
+                out=sums[FILTERS:P, b, 0:IMAGES],
+                in_=acc[b][FILTERS:P, first + IMAGES : first + 2 * IMAGES],
+            )
+
+        result = consts.tile([P, FILTERS, FREQS], F32)
+        per_bank = 4
+        copies = [nc.vector.tensor_copy, nc.scalar.copy]
+        for half in range(PAIRS // per_bank):
+            turned = psum.tile([P, per_bank, P], F32, name="turned%d" % half, tag="acc%d" % half)
+            for k in range(per_bank):
+                nc.tensor.transpose(turned[:, k, :], sums[:, per_bank * half + k, :], identity[:])
+            f0 = 2 * per_bank * half
+            copies[half](
+                out=result[:, :, f0 : f0 + 2 * per_bank].rearrange("p f (k e) -> p f k e", e=2),
+                in_=turned[:].rearrange("p k (e f) -> p f k e", e=2),
+            )
+        flat_out = out.rearrange("n f h w -> n (f h w)")
+        flat_result = result[:].rearrange("p f w -> p (f w)")
+        nc.sync.dma_start(out=flat_out[0:64, :], in_=flat_result[0:64, :])
+        nc.sync.dma_start(out=flat_out[64:IMAGES, :], in_=flat_result[64:IMAGES, :])
+
+
+def window_start(b):
+    return min((2 * IMAGES * b) // STEP * STEP, FREQS * IMAGES - WINDOW)

@@ -22,7 +22,9 @@ HALVES = 2
 WORDS = 4
 RUN = WORDS * PACK * FREQS
 
-ROWS = 8
+K_ROWS = 32
+X_ROWS = 12
+GROUPS = 4
 QUANT_COLS = 1024
 PAIRS = FREQS // 2
 WINDOW = 256
@@ -31,17 +33,24 @@ STEP = 64
 FLOPS = 2 * IMAGES * FILTERS * CHANNELS * FREQS
 
 
-def load_and_regroup(nc, raw_pool, copy, source, quarter, rows, grouped):
+def load_and_regroup(nc, raw_pool, copy, groups_per_copy, source, quarter, rows, rows_per_load, grouped):
     view = source.rearrange(
         "n (s q i c) h w -> q i s n (c h w)", s=SEGMENTS, q=QUARTERS, i=HALVES
     )
-    for r0 in range(0, rows, ROWS):
-        raw = raw_pool.tile([P, ROWS, RUN], BF16)
+    for r0 in range(0, rows, rows_per_load):
+        raw = raw_pool.tile([P, rows_per_load, RUN], BF16)
         for i in range(HALVES):
-            nc.sync.dma_start(out=raw[i:P:HALVES, :, :], in_=view[quarter, i, :, r0 : r0 + ROWS, :])
-        by_word = raw[:].rearrange("p n (j t f) -> p j f n t", j=WORDS, t=PACK)
+            nc.sync.dma_start(
+                out=raw[i:P:HALVES, :, :], in_=view[quarter, i, :, r0 : r0 + rows_per_load, :]
+            )
+        by_word = raw[:].rearrange("p n (j t g i) -> p j g n t i", j=WORDS, t=PACK, g=GROUPS)
         for j in range(WORDS):
-            copy(out=grouped[j][:, :, r0 : r0 + ROWS, :], in_=by_word[:, j])
+            target = grouped[j][:, :, r0 : r0 + rows_per_load, :].rearrange(
+                "p (g i) n t -> p g n t i", g=GROUPS
+            )
+            for g0 in range(0, GROUPS, groups_per_copy):
+                g1 = g0 + groups_per_copy
+                copy(out=target[:, g0:g1], in_=by_word[:, j, g0:g1])
 
 
 def quantise(nc, grouped, codes, scales, cols):
@@ -61,7 +70,8 @@ def tile_convdct_pa_k_kernel(tc, x_dct, k_dct, out):
     k_cols = FREQS * FILTERS
     with ExitStack() as ctx:
         consts = ctx.enter_context(tc.tile_pool(name="consts", bufs=1))
-        raw_pool = ctx.enter_context(tc.tile_pool(name="raw", bufs=16))
+        k_raw = ctx.enter_context(tc.tile_pool(name="k_raw", bufs=3))
+        x_raw = ctx.enter_context(tc.tile_pool(name="x_raw", bufs=8))
         grouped_pool = ctx.enter_context(tc.tile_pool(name="grouped", bufs=5))
         k_mx = ctx.enter_context(tc.tile_pool(name="k_mx", bufs=6))
         x_mx = ctx.enter_context(tc.tile_pool(name="x_mx", bufs=2))
@@ -79,7 +89,7 @@ def tile_convdct_pa_k_kernel(tc, x_dct, k_dct, out):
                 grouped_pool.tile([P, FREQS, FILTERS, PACK], BF16, name="kg%d" % j, tag="kg", align_bytes=64)
                 for j in range(WORDS)
             ]
-            load_and_regroup(nc, raw_pool, nc.scalar.copy, k_dct, q, FILTERS, k_grouped)
+            load_and_regroup(nc, k_raw, nc.scalar.copy, 1, k_dct, q, FILTERS, K_ROWS, k_grouped)
             k_codes = []
             k_scales = []
             for j in range(WORDS):
@@ -93,7 +103,7 @@ def tile_convdct_pa_k_kernel(tc, x_dct, k_dct, out):
                 grouped_pool.tile([P, FREQS, IMAGES, PACK], BF16, name="xg%d" % j, tag="xg", align_bytes=64)
                 for j in range(WORDS)
             ]
-            load_and_regroup(nc, raw_pool, nc.vector.tensor_copy, x_dct, q, IMAGES, x_grouped)
+            load_and_regroup(nc, x_raw, nc.vector.tensor_copy, GROUPS, x_dct, q, IMAGES, X_ROWS, x_grouped)
             for j in range(WORDS):
                 x_codes = x_mx.tile([P, x_cols], U32, align_bytes=64)
                 x_scales = x_mx.tile([P, x_cols], U8, align_bytes=64)

@@ -24,6 +24,7 @@ RUN = WORDS * PACK * FREQS
 
 K_ROWS = 32
 X_ROWS = 12
+DMA_ROWS = 4
 GROUPS = 4
 QUANT_COLS = 1024
 PAIRS = FREQS // 2
@@ -39,10 +40,12 @@ def load_and_regroup(nc, raw_pool, copy, groups_per_copy, source, quarter, rows,
     )
     for r0 in range(0, rows, rows_per_load):
         raw = raw_pool.tile([P, rows_per_load, RUN], BF16)
-        for i in range(HALVES):
-            nc.sync.dma_start(
-                out=raw[i:P:HALVES, :, :], in_=view[quarter, i, :, r0 : r0 + rows_per_load, :]
-            )
+        for d0 in range(0, rows_per_load, DMA_ROWS):
+            for i in range(HALVES):
+                nc.sync.dma_start(
+                    out=raw[i:P:HALVES, d0 : d0 + DMA_ROWS, :],
+                    in_=view[quarter, i, :, r0 + d0 : r0 + d0 + DMA_ROWS, :],
+                )
         by_word = raw[:].rearrange("p n (j t g i) -> p j g n t i", j=WORDS, t=PACK, g=GROUPS)
         for j in range(WORDS):
             target = grouped[j][:, :, r0 : r0 + rows_per_load, :].rearrange(

@@ -24,40 +24,38 @@ RUN = WORDS * PACK * FREQS
 
 K_ROWS = 32
 X_ROWS = 12
-DMA_ROWS = 4
 GROUPS = 4
+OWN_WORDS = 3
 QUANT_COLS = 1024
 PAIRS = FREQS // 2
 WINDOW = 256
 STEP = 64
+PER_BANK = 4
+STORE_CUT = 64
 
 FLOPS = 2 * IMAGES * FILTERS * CHANNELS * FREQS
 
 
-def load_and_regroup(nc, raw_pool, copy, groups_per_copy, source, quarter, rows, rows_per_load, grouped):
+def load(nc, pool, source, q, r0, rows):
     view = source.rearrange(
-        "n (s q i c) h w -> q i s n (c h w)", s=SEGMENTS, q=QUARTERS, i=HALVES
+        "n (s q h c) y x -> q h s n (c y x)", s=SEGMENTS, q=QUARTERS, h=HALVES
     )
-    for r0 in range(0, rows, rows_per_load):
-        raw = raw_pool.tile([P, rows_per_load, RUN], BF16)
-        for d0 in range(0, rows_per_load, DMA_ROWS):
-            for i in range(HALVES):
-                nc.sync.dma_start(
-                    out=raw[i:P:HALVES, d0 : d0 + DMA_ROWS, :],
-                    in_=view[quarter, i, :, r0 + d0 : r0 + d0 + DMA_ROWS, :],
-                )
-        by_word = raw[:].rearrange("p n (j t g i) -> p j g n t i", j=WORDS, t=PACK, g=GROUPS)
-        for j in range(WORDS):
-            target = grouped[j][:, :, r0 : r0 + rows_per_load, :].rearrange(
-                "p (g i) n t -> p g n t i", g=GROUPS
-            )
-            for g0 in range(0, GROUPS, groups_per_copy):
-                g1 = g0 + groups_per_copy
-                copy(out=target[:, g0:g1], in_=by_word[:, j, g0:g1])
+    raw = pool.tile([P, rows, RUN], BF16)
+    for h in range(HALVES):
+        nc.sync.dma_start(out=raw[h:P:HALVES, :, :], in_=view[q, h, :, r0 : r0 + rows, :])
+    return raw
 
 
-def quantise(nc, grouped, codes, scales, cols):
-    flat = grouped[:].rearrange("p f n t -> p (f n t)")
+def regroup(copy, groups_per_copy, raw, j, grouped_word, r0, rows):
+    source = raw[:].rearrange("p n (j t g v) -> p j g n t v", j=WORDS, t=PACK, g=GROUPS)
+    target = grouped_word[:, :, r0 : r0 + rows, :].rearrange("p (g v) n t -> p g n t v", g=GROUPS)
+    for g0 in range(0, GROUPS, groups_per_copy):
+        g1 = g0 + groups_per_copy
+        copy(out=target[:, g0:g1], in_=source[:, j, g0:g1])
+
+
+def quantise(nc, grouped_word, codes, scales, cols):
+    flat = grouped_word[:].rearrange("p w n t -> p (w n t)")
     for c0 in range(0, cols, QUANT_COLS):
         c1 = min(c0 + QUANT_COLS, cols)
         nc.vector.quantize_mx(
@@ -67,18 +65,30 @@ def quantise(nc, grouped, codes, scales, cols):
         )
 
 
+def window_start(b):
+    return min((2 * IMAGES * b) // STEP * STEP, FREQS * IMAGES - WINDOW)
+
+
 def tile_convdct_pa_k_kernel(tc, x_dct, k_dct, out):
     nc = tc.nc
     x_cols = FREQS * IMAGES
     k_cols = FREQS * FILTERS
+
+    def on_vector(raw, j, grouped_word, r0, rows):
+        regroup(nc.vector.tensor_copy, GROUPS, raw, j, grouped_word, r0, rows)
+
+    def on_scalar(raw, j, grouped_word, r0, rows):
+        regroup(nc.scalar.copy, 1, raw, j, grouped_word, r0, rows)
+
     with ExitStack() as ctx:
         consts = ctx.enter_context(tc.tile_pool(name="consts", bufs=1))
         k_raw = ctx.enter_context(tc.tile_pool(name="k_raw", bufs=3))
         x_raw = ctx.enter_context(tc.tile_pool(name="x_raw", bufs=8))
-        grouped_pool = ctx.enter_context(tc.tile_pool(name="grouped", bufs=5))
-        k_mx = ctx.enter_context(tc.tile_pool(name="k_mx", bufs=6))
+        grouped = ctx.enter_context(tc.tile_pool(name="grouped", bufs=WORDS + 1))
+        k_mx = ctx.enter_context(tc.tile_pool(name="k_mx", bufs=WORDS + 2))
         x_mx = ctx.enter_context(tc.tile_pool(name="x_mx", bufs=2))
         psum = ctx.enter_context(tc.psum_pool(name="psum", bufs=1))
+        ctx.enter_context(tc.manual_schedule())
 
         identity = consts.tile([P, P], F32)
         make_identity(nc, identity[:])
@@ -89,24 +99,38 @@ def tile_convdct_pa_k_kernel(tc, x_dct, k_dct, out):
 
         for q in range(QUARTERS):
             k_grouped = [
-                grouped_pool.tile([P, FREQS, FILTERS, PACK], BF16, name="kg%d" % j, tag="kg", align_bytes=64)
+                grouped.tile([P, FREQS, FILTERS, PACK], BF16, name="kg%d" % j, tag="kg", align_bytes=64)
                 for j in range(WORDS)
             ]
-            load_and_regroup(nc, k_raw, nc.scalar.copy, 1, k_dct, q, FILTERS, K_ROWS, k_grouped)
-            k_codes = []
-            k_scales = []
-            for j in range(WORDS):
-                codes = k_mx.tile([P, k_cols], U32, name="kc%d" % j, tag="kc", align_bytes=64)
-                scales = k_mx.tile([P, k_cols], U8, name="ks%d" % j, tag="ks", align_bytes=64)
-                quantise(nc, k_grouped[j], codes, scales, k_cols)
-                k_codes.append(codes)
-                k_scales.append(scales)
+            for r0 in range(0, FILTERS, K_ROWS):
+                raw = load(nc, k_raw, k_dct, q, r0, K_ROWS)
+                for j in range(WORDS):
+                    if j < OWN_WORDS:
+                        on_scalar(raw, j, k_grouped[j], r0, K_ROWS)
+                    else:
+                        on_vector(raw, j, k_grouped[j], r0, K_ROWS)
 
             x_grouped = [
-                grouped_pool.tile([P, FREQS, IMAGES, PACK], BF16, name="xg%d" % j, tag="xg", align_bytes=64)
+                grouped.tile([P, FREQS, IMAGES, PACK], BF16, name="xg%d" % j, tag="xg", align_bytes=64)
                 for j in range(WORDS)
             ]
-            load_and_regroup(nc, x_raw, nc.vector.tensor_copy, GROUPS, x_dct, q, IMAGES, X_ROWS, x_grouped)
+            k_codes = []
+            k_scales = []
+            for r0 in range(0, IMAGES, X_ROWS):
+                raw = load(nc, x_raw, x_dct, q, r0, X_ROWS)
+                for j in range(WORDS):
+                    if j < OWN_WORDS:
+                        on_vector(raw, j, x_grouped[j], r0, X_ROWS)
+                    else:
+                        on_scalar(raw, j, x_grouped[j], r0, X_ROWS)
+                j = len(k_codes)
+                if j < WORDS:
+                    codes = k_mx.tile([P, k_cols], U32, name="kc%d" % j, tag="kc", align_bytes=64)
+                    scales = k_mx.tile([P, k_cols], U8, name="ks%d" % j, tag="ks", align_bytes=64)
+                    quantise(nc, k_grouped[j], codes, scales, k_cols)
+                    k_codes.append(codes)
+                    k_scales.append(scales)
+
             for j in range(WORDS):
                 x_codes = x_mx.tile([P, x_cols], U32, align_bytes=64)
                 x_scales = x_mx.tile([P, x_cols], U8, align_bytes=64)
@@ -125,29 +149,26 @@ def tile_convdct_pa_k_kernel(tc, x_dct, k_dct, out):
 
         for b in range(PAIRS):
             first = 2 * IMAGES * b - window_start(b)
-            nc.vector.tensor_copy(out=sums[0:FILTERS, b, 0:IMAGES], in_=acc[b][0:FILTERS, first : first + IMAGES])
+            nc.vector.tensor_copy(
+                out=sums[0:FILTERS, b, 0:IMAGES], in_=acc[b][0:FILTERS, first : first + IMAGES]
+            )
             nc.scalar.copy(
                 out=sums[FILTERS:P, b, 0:IMAGES],
                 in_=acc[b][FILTERS:P, first + IMAGES : first + 2 * IMAGES],
             )
 
         result = consts.tile([P, FILTERS, FREQS], F32)
-        per_bank = 4
         copies = [nc.vector.tensor_copy, nc.scalar.copy]
-        for half in range(PAIRS // per_bank):
-            turned = psum.tile([P, per_bank, P], F32, name="turned%d" % half, tag="acc%d" % half)
-            for k in range(per_bank):
-                nc.tensor.transpose(turned[:, k, :], sums[:, per_bank * half + k, :], identity[:])
-            f0 = 2 * per_bank * half
+        for half in range(PAIRS // PER_BANK):
+            turned = psum.tile([P, PER_BANK, P], F32, name="turned%d" % half, tag="acc%d" % half)
+            for k in range(PER_BANK):
+                nc.tensor.transpose(turned[:, k, :], sums[:, PER_BANK * half + k, :], identity[:])
+            w0 = 2 * PER_BANK * half
             copies[half](
-                out=result[:, :, f0 : f0 + 2 * per_bank].rearrange("p f (k e) -> p f k e", e=2),
+                out=result[:, :, w0 : w0 + 2 * PER_BANK].rearrange("p f (k e) -> p f k e", e=2),
                 in_=turned[:].rearrange("p k (e f) -> p f k e", e=2),
             )
-        flat_out = out.rearrange("n f h w -> n (f h w)")
+        flat_out = out.rearrange("n f y x -> n (f y x)")
         flat_result = result[:].rearrange("p f w -> p (f w)")
-        nc.sync.dma_start(out=flat_out[0:64, :], in_=flat_result[0:64, :])
-        nc.sync.dma_start(out=flat_out[64:IMAGES, :], in_=flat_result[64:IMAGES, :])
-
-
-def window_start(b):
-    return min((2 * IMAGES * b) // STEP * STEP, FREQS * IMAGES - WINDOW)
+        nc.sync.dma_start(out=flat_out[0:STORE_CUT, :], in_=flat_result[0:STORE_CUT, :])
+        nc.sync.dma_start(out=flat_out[STORE_CUT:IMAGES, :], in_=flat_result[STORE_CUT:IMAGES, :])

@@ -18,157 +18,189 @@ FREQS = 16
 
 SEGMENTS = 64
 QUARTERS = 4
-HALVES = 2
 WORDS = 4
-RUN = WORDS * PACK * FREQS
+HALF = 16 * FREQS
+ROW = QUARTERS * HALF
 
+PIECES = [(1, 0, 0, 1), (0, 1, 0, 2), (1, 3, 1, 2), (0, 5, 2, 2), (1, 7, 3, 1)]
+
+LOAD_ROWS = 8
 K_ROWS = 32
-X_ROWS = 12
+X_ROWS = [32, 24, 16]
 GROUPS = 4
-OWN_WORDS = 3
-QUANT_COLS = 1024
-PAIRS = FREQS // 2
-WINDOW = 256
+PAIR = 2
+QUANT_COLS = [1024, 512, 256]
+BLOCK_FREQS = 4
+BLOCKS = FREQS // BLOCK_FREQS
+WINDOW = 128
 STEP = 64
-PER_BANK = 4
 STORE_CUT = 64
 
 FLOPS = 2 * IMAGES * FILTERS * CHANNELS * FREQS
 
 
-def load(nc, pool, source, q, r0, rows):
-    view = source.rearrange(
-        "n (s q h c) y x -> q h s n (c y x)", s=SEGMENTS, q=QUARTERS, h=HALVES
-    )
-    raw = pool.tile([P, rows, RUN], BF16)
-    for h in range(HALVES):
-        nc.sync.dma_start(out=raw[h:P:HALVES, :, :], in_=view[q, h, :, r0 : r0 + rows, :])
-    return raw
+def load_pieces(nc, source, raw, r0, pieces):
+    view = source.rearrange("n (s c) y x -> s n (c y x)", s=SEGMENTS)
+    for parity, half, q, quarters in pieces:
+        nc.sync.dma_start(
+            out=raw[parity:P:2, :, q * HALF : (q + quarters) * HALF],
+            in_=view[:, r0 : r0 + LOAD_ROWS, half * HALF : (half + quarters) * HALF],
+        )
 
 
-def regroup(copy, groups_per_copy, raw, j, grouped_word, r0, rows):
-    source = raw[:].rearrange("p n (j t g v) -> p j g n t v", j=WORDS, t=PACK, g=GROUPS)
-    target = grouped_word[:, :, r0 : r0 + rows, :].rearrange("p (g v) n t -> p g n t v", g=GROUPS)
+def regroup(copy, groups_per_copy, raw, q, j, grouped, r0):
+    source = raw[:].rearrange("p n (a t g v) -> p a g n t v", a=QUARTERS * WORDS, t=PACK, g=GROUPS)
+    target = grouped[:, j, :, r0 : r0 + LOAD_ROWS, :].rearrange("p (g v) n t -> p g n t v", g=GROUPS)
     for g0 in range(0, GROUPS, groups_per_copy):
         g1 = g0 + groups_per_copy
-        copy(out=target[:, g0:g1], in_=source[:, j, g0:g1])
+        copy(out=target[:, g0:g1], in_=source[:, q * WORDS + j, g0:g1])
 
 
-def quantise(nc, grouped_word, codes, scales, cols):
-    flat = grouped_word[:].rearrange("p w n t -> p (w n t)")
-    for c0 in range(0, cols, QUANT_COLS):
-        c1 = min(c0 + QUANT_COLS, cols)
+def quantise(nc, grouped, pair, codes, scales, cols):
+    flat = grouped[:, PAIR * pair : PAIR * (pair + 1)].rearrange("p j w n t -> p (j w n t)")
+    c0 = 0
+    while c0 < cols:
+        width = max(c for c in QUANT_COLS if c <= cols - c0)
+        c1 = c0 + width
         nc.vector.quantize_mx(
             out=codes[:, c0:c1].bitcast(FP8X4),
             scales=scales[:, c0:c1],
             in_=flat[:, PACK * c0 : PACK * c1],
         )
+        c0 = c1
 
 
-def window_start(b):
-    return min((2 * IMAGES * b) // STEP * STEP, FREQS * IMAGES - WINDOW)
+def window_start(rows, b):
+    return min(BLOCK_FREQS * rows * b // STEP * STEP, FREQS * rows - WINDOW)
 
 
 def tile_convdct_pa_k_kernel(tc, x_dct, k_dct, out):
     nc = tc.nc
-    x_cols = FREQS * IMAGES
-    k_cols = FREQS * FILTERS
-
-    def on_vector(raw, j, grouped_word, r0, rows):
-        regroup(nc.vector.tensor_copy, GROUPS, raw, j, grouped_word, r0, rows)
-
-    def on_scalar(raw, j, grouped_word, r0, rows):
-        regroup(nc.scalar.copy, 1, raw, j, grouped_word, r0, rows)
 
     with ExitStack() as ctx:
         consts = ctx.enter_context(tc.tile_pool(name="consts", bufs=1))
-        k_raw = ctx.enter_context(tc.tile_pool(name="k_raw", bufs=3))
-        x_raw = ctx.enter_context(tc.tile_pool(name="x_raw", bufs=8))
-        grouped = ctx.enter_context(tc.tile_pool(name="grouped", bufs=WORDS + 1))
-        k_mx = ctx.enter_context(tc.tile_pool(name="k_mx", bufs=WORDS + 2))
-        x_mx = ctx.enter_context(tc.tile_pool(name="x_mx", bufs=2))
+        raws = ctx.enter_context(tc.tile_pool(name="raws", bufs=4))
+        groups = ctx.enter_context(tc.tile_pool(name="groups", bufs=QUARTERS))
+        k_mx = ctx.enter_context(tc.tile_pool(name="k_mx", bufs=16))
+        x_mx = ctx.enter_context(tc.tile_pool(name="x_mx", bufs=4))
         psum = ctx.enter_context(tc.psum_pool(name="psum", bufs=1))
         ctx.enter_context(tc.manual_schedule())
 
         identity = consts.tile([P, P], F32)
         make_identity(nc, identity[:])
-        sums = consts.tile([P, PAIRS, P], F32)
+        sums = consts.tile([P, 2 * BLOCKS, P], F32)
         nc.vector.memset(sums[:], 0.0)
 
-        acc = [psum.tile([P, WINDOW], F32, name="acc%d" % b) for b in range(PAIRS)]
+        acc = [psum.tile([P, BLOCKS * P], F32, name="acc%d" % b) for b in range(2 * BLOCKS)]
 
-        for q in range(QUARTERS):
-            k_grouped = [
-                grouped.tile([P, FREQS, FILTERS, PACK], BF16, name="kg%d" % j, tag="kg", align_bytes=64)
-                for j in range(WORDS)
-            ]
-            for r0 in range(0, FILTERS, K_ROWS):
-                raw = load(nc, k_raw, k_dct, q, r0, K_ROWS)
-                for j in range(WORDS):
-                    if j < OWN_WORDS:
-                        on_scalar(raw, j, k_grouped[j], r0, K_ROWS)
-                    else:
-                        on_vector(raw, j, k_grouped[j], r0, K_ROWS)
+        k_tiles = {}
 
-            x_grouped = [
-                grouped.tile([P, FREQS, IMAGES, PACK], BF16, name="xg%d" % j, tag="xg", align_bytes=64)
-                for j in range(WORDS)
-            ]
-            k_codes = []
-            k_scales = []
-            for r0 in range(0, IMAGES, X_ROWS):
-                raw = load(nc, x_raw, x_dct, q, r0, X_ROWS)
-                for j in range(WORDS):
-                    if j < OWN_WORDS:
-                        on_vector(raw, j, x_grouped[j], r0, X_ROWS)
-                    else:
-                        on_scalar(raw, j, x_grouped[j], r0, X_ROWS)
-                j = len(k_codes)
-                if j < WORDS:
-                    codes = k_mx.tile([P, k_cols], U32, name="kc%d" % j, tag="kc", align_bytes=64)
-                    scales = k_mx.tile([P, k_cols], U8, name="ks%d" % j, tag="ks", align_bytes=64)
-                    quantise(nc, k_grouped[j], codes, scales, k_cols)
-                    k_codes.append(codes)
-                    k_scales.append(scales)
-
+        def copies(raw, q, grouped, r0):
             for j in range(WORDS):
-                x_codes = x_mx.tile([P, x_cols], U32, align_bytes=64)
-                x_scales = x_mx.tile([P, x_cols], U8, align_bytes=64)
-                quantise(nc, x_grouped[j], x_codes, x_scales, x_cols)
-                for b in range(PAIRS):
-                    w0 = window_start(b)
-                    nc.tensor.matmul_mx(
-                        out=acc[b][:],
-                        lhsT=k_codes[j][:, P * b : P * (b + 1)].bitcast(FP8X4),
-                        lhsT_scale=k_scales[j][:, P * b : P * (b + 1)],
-                        rhs=x_codes[:, w0 : w0 + WINDOW].bitcast(FP8X4),
-                        rhs_scale=x_scales[:, w0 : w0 + WINDOW],
-                        start=(q == 0 and j == 0),
-                        stop=(q == QUARTERS - 1 and j == WORDS - 1),
+                if j < PAIR:
+                    regroup(nc.vector.tensor_copy, GROUPS, raw, q, j, grouped, r0)
+                else:
+                    regroup(nc.scalar.copy, 1, raw, q, j, grouped, r0)
+
+        def quantise_k(chunk, q, grouped):
+            cols = PAIR * FREQS * K_ROWS
+            for pair in range(WORDS // PAIR):
+                codes = k_mx.tile([P, cols], U32, name="kc", tag="kc", align_bytes=64)
+                scales = k_mx.tile([P, cols], U8, name="ks", tag="ks", align_bytes=64)
+                quantise(nc, grouped, pair, codes, scales, cols)
+                k_tiles[chunk, q, pair] = (codes, scales)
+
+        def multiply(q, grouped, rows):
+            cols = PAIR * FREQS * rows
+            for pair in range(WORDS // PAIR):
+                codes = x_mx.tile([P, cols], U32, name="xc", tag="xc", align_bytes=64)
+                scales = x_mx.tile([P, cols], U8, name="xs", tag="xs", align_bytes=64)
+                quantise(nc, grouped, pair, codes, scales, cols)
+                for i in range(PAIR):
+                    for s in range(2 * BLOCKS):
+                        chunk, b = divmod(s, BLOCKS)
+                        k_codes, k_scales = k_tiles[chunk, q, pair]
+                        k0 = FREQS * K_ROWS * i + P * b
+                        x0 = FREQS * rows * i + window_start(rows, b)
+                        nc.tensor.matmul_mx(
+                            out=acc[s][:, 0:WINDOW],
+                            lhsT=k_codes[:, k0 : k0 + P].bitcast(FP8X4),
+                            lhsT_scale=k_scales[:, k0 : k0 + P],
+                            rhs=codes[:, x0 : x0 + WINDOW].bitcast(FP8X4),
+                            rhs_scale=scales[:, x0 : x0 + WINDOW],
+                            start=(q == 0 and pair == 0 and i == 0),
+                            stop=(q == QUARTERS - 1 and pair == WORDS // PAIR - 1 and i == PAIR - 1),
+                        )
+
+        def empty(n0, rows):
+            for s in range(2 * BLOCKS):
+                b = s % BLOCKS
+                copy = nc.vector.tensor_copy if s % 2 == 0 else nc.scalar.copy
+                for e in range(BLOCK_FREQS):
+                    first = rows * (BLOCK_FREQS * b + e) - window_start(rows, b)
+                    part = slice(K_ROWS * e, K_ROWS * (e + 1))
+                    copy(out=sums[part, s, n0 : n0 + rows], in_=acc[s][part, first : first + rows])
+
+        sections = [(k_dct, K_ROWS * chunk, K_ROWS, chunk) for chunk in range(FILTERS // K_ROWS)]
+        n0 = 0
+        for rows in X_ROWS:
+            sections.append((x_dct, n0, rows, None))
+            n0 += rows
+
+        late = []
+        to_empty = []
+        for index, (source, first, rows, chunk) in enumerate(sections):
+            loads = rows // LOAD_ROWS
+            grouped = []
+            if index == len(sections) - 1:
+                raw = [raws.tile([P, LOAD_ROWS, ROW], BF16, name="raw", tag="raw") for i in range(loads)]
+                for piece in PIECES:
+                    for i in range(loads):
+                        load_pieces(nc, source, raw[i], first + LOAD_ROWS * i, [piece])
+                steps = [(i, q) for q in range(QUARTERS) for i in range(loads)]
+            else:
+                raw = []
+                steps = [(i, q) for i in range(loads) for q in range(QUARTERS)]
+            for i, q in steps:
+                if i == len(raw):
+                    raw.append(raws.tile([P, LOAD_ROWS, ROW], BF16, name="raw", tag="raw"))
+                    load_pieces(nc, source, raw[i], first + LOAD_ROWS * i, PIECES)
+                if q == len(grouped):
+                    grouped.append(
+                        groups.tile([P, WORDS, FREQS, rows, PACK], BF16, name="grouped", tag="grouped", align_bytes=64)
                     )
+                copies(raw[i], q, grouped[q], LOAD_ROWS * i)
+                for work in late:
+                    work()
+                late = []
+                if i == loads - 1:
+                    if chunk is not None:
+                        late.append(lambda chunk=chunk, q=q, tile=grouped[q]: quantise_k(chunk, q, tile))
+                    else:
+                        if q == 0:
+                            for done in to_empty:
+                                empty(done[0], done[1])
+                            to_empty = [(first, rows)]
+                        late.append(lambda q=q, tile=grouped[q], rows=rows: multiply(q, tile, rows))
+        for work in late:
+            work()
+        for done in to_empty:
+            empty(done[0], done[1])
 
-        for b in range(PAIRS):
-            first = 2 * IMAGES * b - window_start(b)
-            nc.vector.tensor_copy(
-                out=sums[0:FILTERS, b, 0:IMAGES], in_=acc[b][0:FILTERS, first : first + IMAGES]
-            )
-            nc.scalar.copy(
-                out=sums[FILTERS:P, b, 0:IMAGES],
-                in_=acc[b][FILTERS:P, first + IMAGES : first + 2 * IMAGES],
-            )
-
-        result = consts.tile([P, FILTERS, FREQS], F32)
-        copies = [nc.vector.tensor_copy, nc.scalar.copy]
-        for half in range(PAIRS // PER_BANK):
-            turned = psum.tile([P, PER_BANK, P], F32, name="turned%d" % half, tag="acc%d" % half)
-            for k in range(PER_BANK):
-                nc.tensor.transpose(turned[:, k, :], sums[:, PER_BANK * half + k, :], identity[:])
-            w0 = 2 * PER_BANK * half
-            copies[half](
-                out=result[:, :, w0 : w0 + 2 * PER_BANK].rearrange("p f (k e) -> p f k e", e=2),
-                in_=turned[:].rearrange("p k (e f) -> p f k e", e=2),
-            )
+        result = groups.tile([P, FILTERS, FREQS], F32, name="result", tag="grouped", align_bytes=64)
         flat_out = out.rearrange("n f y x -> n (f y x)")
-        flat_result = result[:].rearrange("p f w -> p (f w)")
-        nc.sync.dma_start(out=flat_out[0:STORE_CUT, :], in_=flat_result[0:STORE_CUT, :])
-        nc.sync.dma_start(out=flat_out[STORE_CUT:IMAGES, :], in_=flat_result[STORE_CUT:IMAGES, :])
+        turn_copies = [nc.vector.tensor_copy, nc.scalar.copy]
+        for chunk in range(2):
+            turned = psum.tile([P, BLOCKS, P], F32, name="turned%d" % chunk, tag="acc%d" % chunk)
+            for b in range(BLOCKS):
+                nc.tensor.transpose(turned[:, b, :], sums[:, BLOCKS * chunk + b, :], identity[:])
+            f0 = K_ROWS * chunk
+            turn_copies[chunk](
+                out=result[0:IMAGES, f0 : f0 + K_ROWS, :].rearrange("p f (b e) -> p f b e", e=BLOCK_FREQS),
+                in_=turned[0:IMAGES].rearrange("p b (e f) -> p f b e", e=BLOCK_FREQS),
+            )
+            flat = result[:, f0 : f0 + K_ROWS, :].rearrange("p f w -> p (f w)")
+            w0 = f0 * FREQS
+            w1 = w0 + K_ROWS * FREQS
+            nc.sync.dma_start(out=flat_out[0:STORE_CUT, w0:w1], in_=flat[0:STORE_CUT, :])
+            nc.sync.dma_start(out=flat_out[STORE_CUT:IMAGES, w0:w1], in_=flat[STORE_CUT:IMAGES, :])

@@ -28,6 +28,7 @@ LOAD_ROWS = 8
 K_ROWS = 32
 X_ROWS = [32, 24, 16]
 GROUPS = 4
+VECTOR_WORDS = [2, 3, 2, 3]
 PAIR = 2
 QUANT_COLS = [1024, 512, 256]
 BLOCK_FREQS = 4
@@ -97,7 +98,7 @@ def tile_convdct_pa_k_kernel(tc, x_dct, k_dct, out):
 
         def copies(raw, q, grouped, r0):
             for j in range(WORDS):
-                if j < PAIR:
+                if j < VECTOR_WORDS[q]:
                     regroup(nc.vector.tensor_copy, GROUPS, raw, q, j, grouped, r0)
                 else:
                     regroup(nc.scalar.copy, 1, raw, q, j, grouped, r0)

@@ -99,7 +99,7 @@ def tile_convdct_pa_k_kernel(tc, x_dct, k_dct, out):
         def copies(raw, q, grouped, r0):
             for j in range(WORDS):
                 if j < VECTOR_WORDS[q]:
-                    regroup(nc.vector.tensor_copy, GROUPS, raw, q, j, grouped, r0)
+                    regroup(nc.vector.tensor_copy, 1, raw, q, j, grouped, r0)
                 else:
                     regroup(nc.scalar.copy, 1, raw, q, j, grouped, r0)
 

@@ -25,10 +25,14 @@ ROW = QUARTERS * HALF
 PIECES = [(1, 0, 0, 1), (0, 1, 0, 2), (1, 3, 1, 2), (0, 5, 2, 2), (1, 7, 3, 1)]
 
 LOAD_ROWS = 8
+RING_ROWS = 32
+CHUNK_ROWS = 16
 K_ROWS = 32
-X_ROWS = [32, 24, 16]
+X_ROWS = [32, 16, 24]
 GROUPS = 4
-VECTOR_WORDS = [2, 3, 2, 3]
+VECTOR_WORDS = [2, 2, 2, 2]
+VECTOR_WORDS_ALONE = [3, 2, 3, 2]
+VECTOR_WORDS_END = [2, 2, 2, 3]
 PAIR = 2
 QUANT_COLS = [1024, 512, 256]
 BLOCK_FREQS = 4
@@ -40,21 +44,22 @@ STORE_CUT = 64
 FLOPS = 2 * IMAGES * FILTERS * CHANNELS * FREQS
 
 
-def load_pieces(nc, source, raw, r0, pieces):
+def load_piece(nc, source, ring, slot, r0, piece):
+    parity, half, q, quarters = piece
     view = source.rearrange("n (s c) y x -> s n (c y x)", s=SEGMENTS)
-    for parity, half, q, quarters in pieces:
-        nc.sync.dma_start(
-            out=raw[parity:P:2, :, q * HALF : (q + quarters) * HALF],
-            in_=view[:, r0 : r0 + LOAD_ROWS, half * HALF : (half + quarters) * HALF],
-        )
+    nc.sync.dma_start(
+        out=ring[parity:P:2, slot : slot + LOAD_ROWS, q * HALF : (q + quarters) * HALF],
+        in_=view[:, r0 : r0 + LOAD_ROWS, half * HALF : (half + quarters) * HALF],
+    )
 
 
-def regroup(copy, groups_per_copy, raw, q, j, grouped, r0):
-    source = raw[:].rearrange("p n (a t g v) -> p a g n t v", a=QUARTERS * WORDS, t=PACK, g=GROUPS)
-    target = grouped[:, j, :, r0 : r0 + LOAD_ROWS, :].rearrange("p (g v) n t -> p g n t v", g=GROUPS)
-    for g0 in range(0, GROUPS, groups_per_copy):
-        g1 = g0 + groups_per_copy
-        copy(out=target[:, g0:g1], in_=source[:, q * WORDS + j, g0:g1])
+def regroup(copy, ring, slot, rows, q, j, grouped, r0):
+    source = ring[:, slot : slot + rows, :].rearrange(
+        "p n (a t g v) -> p a g n t v", a=QUARTERS * WORDS, t=PACK, g=GROUPS
+    )
+    target = grouped[:, j, :, r0 : r0 + rows, :].rearrange("p (g v) n t -> p g n t v", g=GROUPS)
+    for g in range(GROUPS):
+        copy(out=target[:, g], in_=source[:, q * WORDS + j, g])
 
 
 def quantise(nc, grouped, pair, codes, scales, cols):
@@ -80,7 +85,6 @@ def tile_convdct_pa_k_kernel(tc, x_dct, k_dct, out):
 
     with ExitStack() as ctx:
         consts = ctx.enter_context(tc.tile_pool(name="consts", bufs=1))
-        raws = ctx.enter_context(tc.tile_pool(name="raws", bufs=4))
         groups = ctx.enter_context(tc.tile_pool(name="groups", bufs=QUARTERS))
         k_mx = ctx.enter_context(tc.tile_pool(name="k_mx", bufs=16))
         x_mx = ctx.enter_context(tc.tile_pool(name="x_mx", bufs=4))
@@ -91,17 +95,16 @@ def tile_convdct_pa_k_kernel(tc, x_dct, k_dct, out):
         make_identity(nc, identity[:])
         sums = consts.tile([P, 2 * BLOCKS, P], F32)
         nc.vector.memset(sums[:], 0.0)
+        ring = consts.tile([P, RING_ROWS, ROW], BF16)
 
         acc = [psum.tile([P, BLOCKS * P], F32, name="acc%d" % b) for b in range(2 * BLOCKS)]
 
         k_tiles = {}
 
-        def copies(raw, q, grouped, r0):
+        def copies(slot, rows, q, grouped, r0, vector_words):
             for j in range(WORDS):
-                if j < VECTOR_WORDS[q]:
-                    regroup(nc.vector.tensor_copy, 1, raw, q, j, grouped, r0)
-                else:
-                    regroup(nc.scalar.copy, 1, raw, q, j, grouped, r0)
+                copy = nc.vector.tensor_copy if j < vector_words[q] else nc.scalar.copy
+                regroup(copy, ring, slot, rows, q, j, grouped, r0)
 
         def quantise_k(chunk, q, grouped):
             cols = PAIR * FREQS * K_ROWS
@@ -111,7 +114,7 @@ def tile_convdct_pa_k_kernel(tc, x_dct, k_dct, out):
                 quantise(nc, grouped, pair, codes, scales, cols)
                 k_tiles[chunk, q, pair] = (codes, scales)
 
-        def multiply(q, grouped, rows):
+        def multiply(q, grouped, rows, out0):
             cols = PAIR * FREQS * rows
             for pair in range(WORDS // PAIR):
                 codes = x_mx.tile([P, cols], U32, name="xc", tag="xc", align_bytes=64)
@@ -124,7 +127,7 @@ def tile_convdct_pa_k_kernel(tc, x_dct, k_dct, out):
                         k0 = FREQS * K_ROWS * i + P * b
                         x0 = FREQS * rows * i + window_start(rows, b)
                         nc.tensor.matmul_mx(
-                            out=acc[s][:, 0:WINDOW],
+                            out=acc[s][:, out0 : out0 + WINDOW],
                             lhsT=k_codes[:, k0 : k0 + P].bitcast(FP8X4),
                             lhsT_scale=k_scales[:, k0 : k0 + P],
                             rhs=codes[:, x0 : x0 + WINDOW].bitcast(FP8X4),
@@ -133,12 +136,12 @@ def tile_convdct_pa_k_kernel(tc, x_dct, k_dct, out):
                             stop=(q == QUARTERS - 1 and pair == WORDS // PAIR - 1 and i == PAIR - 1),
                         )
 
-        def empty(n0, rows):
+        def empty(n0, rows, out0):
             for s in range(2 * BLOCKS):
                 b = s % BLOCKS
                 copy = nc.vector.tensor_copy if s % 2 == 0 else nc.scalar.copy
                 for e in range(BLOCK_FREQS):
-                    first = rows * (BLOCK_FREQS * b + e) - window_start(rows, b)
+                    first = out0 + rows * (BLOCK_FREQS * b + e) - window_start(rows, b)
                     part = slice(K_ROWS * e, K_ROWS * (e + 1))
                     copy(out=sums[part, s, n0 : n0 + rows], in_=acc[s][part, first : first + rows])
 
@@ -150,43 +153,54 @@ def tile_convdct_pa_k_kernel(tc, x_dct, k_dct, out):
 
         late = []
         to_empty = []
+        loaded = 0
         for index, (source, first, rows, chunk) in enumerate(sections):
-            loads = rows // LOAD_ROWS
+            is_last = index == len(sections) - 1
+            chunks = []
+            for r0 in range(0, rows, CHUNK_ROWS):
+                chunks.append((r0, min(CHUNK_ROWS, rows - r0), (loaded + r0) % RING_ROWS))
+            loaded += rows
+            batches = [chunks] if is_last else [[one] for one in chunks]
+            out0 = WINDOW if is_last else 0
             grouped = []
-            if index == len(sections) - 1:
-                raw = [raws.tile([P, LOAD_ROWS, ROW], BF16, name="raw", tag="raw") for i in range(loads)]
+            for batch in batches:
                 for piece in PIECES:
-                    for i in range(loads):
-                        load_pieces(nc, source, raw[i], first + LOAD_ROWS * i, [piece])
-                steps = [(i, q) for q in range(QUARTERS) for i in range(loads)]
-            else:
-                raw = []
-                steps = [(i, q) for i in range(loads) for q in range(QUARTERS)]
-            for i, q in steps:
-                if i == len(raw):
-                    raw.append(raws.tile([P, LOAD_ROWS, ROW], BF16, name="raw", tag="raw"))
-                    load_pieces(nc, source, raw[i], first + LOAD_ROWS * i, PIECES)
-                if q == len(grouped):
-                    grouped.append(
-                        groups.tile([P, WORDS, FREQS, rows, PACK], BF16, name="grouped", tag="grouped", align_bytes=64)
-                    )
-                copies(raw[i], q, grouped[q], LOAD_ROWS * i)
-                for work in late:
-                    work()
-                late = []
-                if i == loads - 1:
-                    if chunk is not None:
-                        late.append(lambda chunk=chunk, q=q, tile=grouped[q]: quantise_k(chunk, q, tile))
-                    else:
-                        if q == 0:
-                            for done in to_empty:
-                                empty(done[0], done[1])
-                            to_empty = [(first, rows)]
-                        late.append(lambda q=q, tile=grouped[q], rows=rows: multiply(q, tile, rows))
+                    for r0, count, slot in batch:
+                        for i in range(0, count, LOAD_ROWS):
+                            load_piece(nc, source, ring, slot + i, first + r0 + i, piece)
+                ends = batch[-1] == chunks[-1]
+                for q in range(QUARTERS):
+                    if q == len(grouped):
+                        grouped.append(
+                            groups.tile([P, WORDS, FREQS, rows, PACK], BF16, name="grouped", tag="grouped", align_bytes=64)
+                        )
+                    for step, (r0, count, slot) in enumerate(batch):
+                        if is_last:
+                            vector_words = VECTOR_WORDS_END
+                        else:
+                            vector_words = VECTOR_WORDS if ends else VECTOR_WORDS_ALONE
+                        copies(slot, count, q, grouped[q], r0, vector_words)
+                        if step == 0:
+                            for work in late:
+                                work()
+                            late = []
+                    if ends:
+                        if chunk is not None:
+                            late.append(lambda chunk=chunk, q=q, tile=grouped[q]: quantise_k(chunk, q, tile))
+                        else:
+                            if q == 0:
+                                if not is_last:
+                                    for done in to_empty:
+                                        empty(done[0], done[1], done[2])
+                                    to_empty = []
+                                to_empty.append((first, rows, out0))
+                            late.append(
+                                lambda q=q, tile=grouped[q], rows=rows, out0=out0: multiply(q, tile, rows, out0)
+                            )
         for work in late:
             work()
         for done in to_empty:
-            empty(done[0], done[1])
+            empty(done[0], done[1], done[2])
 
         result = groups.tile([P, FILTERS, FREQS], F32, name="result", tag="grouped", align_bytes=64)
         flat_out = out.rearrange("n f y x -> n (f y x)")

@@ -24,16 +24,13 @@ ROW = QUARTERS * HALF
 
 PIECES = [(1, 0, 0, 1), (0, 1, 0, 2), (1, 3, 1, 2), (0, 5, 2, 2), (1, 7, 3, 1)]
 
-LOAD_ROWS = 8
 RING_ROWS = 32
-CHUNK_ROWS = 16
+FIRST_LOADS = [8, 8, 16]
 K_ROWS = 32
-X_ROWS = [32, 16, 24]
+X_ROWS = [32, 24, 16]
 GROUPS = 4
-VECTOR_WORDS = [2, 2, 2, 2]
-VECTOR_WORDS_ALONE = [3, 2, 3, 2]
-VECTOR_WORDS_END = [2, 2, 2, 3]
 PAIR = 2
+PAIRS = WORDS // PAIR
 QUANT_COLS = [1024, 512, 256]
 BLOCK_FREQS = 4
 BLOCKS = FREQS // BLOCK_FREQS
@@ -44,13 +41,13 @@ STORE_CUT = 64
 FLOPS = 2 * IMAGES * FILTERS * CHANNELS * FREQS
 
 
-def load_piece(nc, source, ring, slot, r0, piece):
-    parity, half, q, quarters = piece
+def load(nc, source, ring, slot, rows, r0):
     view = source.rearrange("n (s c) y x -> s n (c y x)", s=SEGMENTS)
-    nc.sync.dma_start(
-        out=ring[parity:P:2, slot : slot + LOAD_ROWS, q * HALF : (q + quarters) * HALF],
-        in_=view[:, r0 : r0 + LOAD_ROWS, half * HALF : (half + quarters) * HALF],
-    )
+    for parity, half, q, quarters in PIECES:
+        nc.sync.dma_start(
+            out=ring[parity:P:2, slot : slot + rows, q * HALF : (q + quarters) * HALF],
+            in_=view[:, r0 : r0 + rows, half * HALF : (half + quarters) * HALF],
+        )
 
 
 def regroup(copy, ring, slot, rows, q, j, grouped, r0):
@@ -95,53 +92,53 @@ def tile_convdct_pa_k_kernel(tc, x_dct, k_dct, out):
         make_identity(nc, identity[:])
         sums = consts.tile([P, 2 * BLOCKS, P], F32)
         nc.vector.memset(sums[:], 0.0)
+        warm = consts.tile([P, 1], F32)
+        nc.scalar.copy(out=warm[:], in_=sums[:, 0, 0:1])
         ring = consts.tile([P, RING_ROWS, ROW], BF16)
 
         acc = [psum.tile([P, BLOCKS * P], F32, name="acc%d" % b) for b in range(2 * BLOCKS)]
 
         k_tiles = {}
 
-        def copies(slot, rows, q, grouped, r0, vector_words):
+        def copies(slot, rows, q, grouped, r0):
             for j in range(WORDS):
-                copy = nc.vector.tensor_copy if j < vector_words[q] else nc.scalar.copy
+                copy = nc.vector.tensor_copy if j < PAIR else nc.scalar.copy
                 regroup(copy, ring, slot, rows, q, j, grouped, r0)
 
-        def quantise_k(chunk, q, grouped):
+        def quantise_k(chunk, q, pair, grouped):
             cols = PAIR * FREQS * K_ROWS
-            for pair in range(WORDS // PAIR):
-                codes = k_mx.tile([P, cols], U32, name="kc", tag="kc", align_bytes=64)
-                scales = k_mx.tile([P, cols], U8, name="ks", tag="ks", align_bytes=64)
-                quantise(nc, grouped, pair, codes, scales, cols)
-                k_tiles[chunk, q, pair] = (codes, scales)
+            codes = k_mx.tile([P, cols], U32, name="kc", tag="kc", align_bytes=64)
+            scales = k_mx.tile([P, cols], U8, name="ks", tag="ks", align_bytes=64)
+            quantise(nc, grouped, pair, codes, scales, cols)
+            k_tiles[chunk, q, pair] = (codes, scales)
 
-        def multiply(q, grouped, rows, out0):
+        def multiply(q, pair, grouped, rows):
             cols = PAIR * FREQS * rows
-            for pair in range(WORDS // PAIR):
-                codes = x_mx.tile([P, cols], U32, name="xc", tag="xc", align_bytes=64)
-                scales = x_mx.tile([P, cols], U8, name="xs", tag="xs", align_bytes=64)
-                quantise(nc, grouped, pair, codes, scales, cols)
-                for i in range(PAIR):
-                    for s in range(2 * BLOCKS):
-                        chunk, b = divmod(s, BLOCKS)
-                        k_codes, k_scales = k_tiles[chunk, q, pair]
-                        k0 = FREQS * K_ROWS * i + P * b
-                        x0 = FREQS * rows * i + window_start(rows, b)
-                        nc.tensor.matmul_mx(
-                            out=acc[s][:, out0 : out0 + WINDOW],
-                            lhsT=k_codes[:, k0 : k0 + P].bitcast(FP8X4),
-                            lhsT_scale=k_scales[:, k0 : k0 + P],
-                            rhs=codes[:, x0 : x0 + WINDOW].bitcast(FP8X4),
-                            rhs_scale=scales[:, x0 : x0 + WINDOW],
-                            start=(q == 0 and pair == 0 and i == 0),
-                            stop=(q == QUARTERS - 1 and pair == WORDS // PAIR - 1 and i == PAIR - 1),
-                        )
+            codes = x_mx.tile([P, cols], U32, name="xc", tag="xc", align_bytes=64)
+            scales = x_mx.tile([P, cols], U8, name="xs", tag="xs", align_bytes=64)
+            quantise(nc, grouped, pair, codes, scales, cols)
+            for i in range(PAIR):
+                for s in range(2 * BLOCKS):
+                    chunk, b = divmod(s, BLOCKS)
+                    k_codes, k_scales = k_tiles[chunk, q, pair]
+                    k0 = FREQS * K_ROWS * i + P * b
+                    x0 = FREQS * rows * i + window_start(rows, b)
+                    nc.tensor.matmul_mx(
+                        out=acc[s][:, 0:WINDOW],
+                        lhsT=k_codes[:, k0 : k0 + P].bitcast(FP8X4),
+                        lhsT_scale=k_scales[:, k0 : k0 + P],
+                        rhs=codes[:, x0 : x0 + WINDOW].bitcast(FP8X4),
+                        rhs_scale=scales[:, x0 : x0 + WINDOW],
+                        start=(q == 0 and pair == 0 and i == 0),
+                        stop=(q == QUARTERS - 1 and pair == PAIRS - 1 and i == PAIR - 1),
+                    )
 
-        def empty(n0, rows, out0):
+        def empty(n0, rows):
             for s in range(2 * BLOCKS):
                 b = s % BLOCKS
                 copy = nc.vector.tensor_copy if s % 2 == 0 else nc.scalar.copy
                 for e in range(BLOCK_FREQS):
-                    first = out0 + rows * (BLOCK_FREQS * b + e) - window_start(rows, b)
+                    first = rows * (BLOCK_FREQS * b + e) - window_start(rows, b)
                     part = slice(K_ROWS * e, K_ROWS * (e + 1))
                     copy(out=sums[part, s, n0 : n0 + rows], in_=acc[s][part, first : first + rows])
 
@@ -153,54 +150,40 @@ def tile_convdct_pa_k_kernel(tc, x_dct, k_dct, out):
 
         late = []
         to_empty = []
-        loaded = 0
         for index, (source, first, rows, chunk) in enumerate(sections):
             is_last = index == len(sections) - 1
-            chunks = []
-            for r0 in range(0, rows, CHUNK_ROWS):
-                chunks.append((r0, min(CHUNK_ROWS, rows - r0), (loaded + r0) % RING_ROWS))
-            loaded += rows
-            batches = [chunks] if is_last else [[one] for one in chunks]
-            out0 = WINDOW if is_last else 0
             grouped = []
-            for batch in batches:
-                for piece in PIECES:
-                    for r0, count, slot in batch:
-                        for i in range(0, count, LOAD_ROWS):
-                            load_piece(nc, source, ring, slot + i, first + r0 + i, piece)
-                ends = batch[-1] == chunks[-1]
+            r0 = 0
+            for batch_rows in FIRST_LOADS if index == 0 else [rows]:
+                slot = RING_ROWS - rows + r0
+                load(nc, source, ring, slot, batch_rows, first + r0)
                 for q in range(QUARTERS):
                     if q == len(grouped):
                         grouped.append(
                             groups.tile([P, WORDS, FREQS, rows, PACK], BF16, name="grouped", tag="grouped", align_bytes=64)
                         )
-                    for step, (r0, count, slot) in enumerate(batch):
-                        if is_last:
-                            vector_words = VECTOR_WORDS_END
-                        else:
-                            vector_words = VECTOR_WORDS if ends else VECTOR_WORDS_ALONE
-                        copies(slot, count, q, grouped[q], r0, vector_words)
-                        if step == 0:
-                            for work in late:
-                                work()
-                            late = []
-                    if ends:
-                        if chunk is not None:
-                            late.append(lambda chunk=chunk, q=q, tile=grouped[q]: quantise_k(chunk, q, tile))
-                        else:
-                            if q == 0:
-                                if not is_last:
-                                    for done in to_empty:
-                                        empty(done[0], done[1], done[2])
-                                    to_empty = []
-                                to_empty.append((first, rows, out0))
-                            late.append(
-                                lambda q=q, tile=grouped[q], rows=rows, out0=out0: multiply(q, tile, rows, out0)
-                            )
-        for work in late:
-            work()
+                    copies(slot, batch_rows, q, grouped[q], r0)
+                    if r0 + batch_rows < rows:
+                        continue
+                    for work in late:
+                        work()
+                    if chunk is not None:
+                        quantise_k(chunk, q, 0, grouped[q])
+                        late = [lambda chunk=chunk, q=q, tile=grouped[q]: quantise_k(chunk, q, 1, tile)]
+                    else:
+                        if q == 0:
+                            for done in to_empty:
+                                empty(done[0], done[1])
+                            to_empty = [(first, rows)]
+                        multiply(q, 0, grouped[q], rows)
+                        late = [lambda q=q, tile=grouped[q], rows=rows: multiply(q, 1, tile, rows)]
+                    if is_last or q == QUARTERS - 1:
+                        for work in late:
+                            work()
+                        late = []
+                r0 += batch_rows
         for done in to_empty:
-            empty(done[0], done[1], done[2])
+            empty(done[0], done[1])
 
         result = groups.tile([P, FILTERS, FREQS], F32, name="result", tag="grouped", align_bytes=64)
         flat_out = out.rearrange("n f y x -> n (f y x)")

from contextlib import ExitStack

import concourse.mybir as mybir
from concourse.masks import make_identity

BF16 = mybir.dt.bfloat16
F32 = mybir.dt.float32
U32 = mybir.dt.uint32
U8 = mybir.dt.uint8
FP8X4 = mybir.dt.float8_e4m3fn_x4

P = 128
PACK = 4
IMAGES = 72
FILTERS = 64
CHANNELS = 8192
FREQS = 16

SEGMENTS = 64
QUARTERS = 4
WORDS = 4
HALF = 16 * FREQS
ROW = QUARTERS * HALF

PIECES = [(1, 0, 0, 1), (0, 1, 0, 2), (1, 3, 1, 2), (0, 5, 2, 2), (1, 7, 3, 1)]

RING_ROWS = 32
FIRST_LOADS = [8, 8, 16]
K_ROWS = 32
X_ROWS = [32, 24, 16]
GROUPS = 4
PAIR = 2
PAIRS = WORDS // PAIR
QUANT_COLS = [1024, 512, 256]
BLOCK_FREQS = 4
BLOCKS = FREQS // BLOCK_FREQS
WINDOW = 128
STEP = 64
STORE_CUT = 64

FLOPS = 2 * IMAGES * FILTERS * CHANNELS * FREQS


def load(nc, source, ring, slot, rows, r0):
    view = source.rearrange("n (s c) y x -> s n (c y x)", s=SEGMENTS)
    for parity, half, q, quarters in PIECES:
        nc.sync.dma_start(
            out=ring[parity:P:2, slot : slot + rows, q * HALF : (q + quarters) * HALF],
            in_=view[:, r0 : r0 + rows, half * HALF : (half + quarters) * HALF],
        )


def regroup(copy, ring, slot, rows, q, j, grouped, r0):
    source = ring[:, slot : slot + rows, :].rearrange(
        "p n (a t g v) -> p a g n t v", a=QUARTERS * WORDS, t=PACK, g=GROUPS
    )
    target = grouped[:, j, :, r0 : r0 + rows, :].rearrange("p (g v) n t -> p g n t v", g=GROUPS)
    for g in range(GROUPS):
        copy(out=target[:, g], in_=source[:, q * WORDS + j, g])


def quantise(nc, grouped, pair, codes, scales, cols):
    flat = grouped[:, PAIR * pair : PAIR * (pair + 1)].rearrange("p j w n t -> p (j w n t)")
    c0 = 0
    while c0 < cols:
        width = max(c for c in QUANT_COLS if c <= cols - c0)
        c1 = c0 + width
        nc.vector.quantize_mx(
            out=codes[:, c0:c1].bitcast(FP8X4),
            scales=scales[:, c0:c1],
            in_=flat[:, PACK * c0 : PACK * c1],
        )
        c0 = c1


def window_start(rows, b):
    return min(BLOCK_FREQS * rows * b // STEP * STEP, FREQS * rows - WINDOW)


def tile_convdct_pa_k_kernel(tc, x_dct, k_dct, out):
    nc = tc.nc

    with ExitStack() as ctx:
        consts = ctx.enter_context(tc.tile_pool(name="consts", bufs=1))
        groups = ctx.enter_context(tc.tile_pool(name="groups", bufs=QUARTERS))
        k_mx = ctx.enter_context(tc.tile_pool(name="k_mx", bufs=16))
        x_mx = ctx.enter_context(tc.tile_pool(name="x_mx", bufs=4))
        psum = ctx.enter_context(tc.psum_pool(name="psum", bufs=1))
        ctx.enter_context(tc.manual_schedule())

        identity = consts.tile([P, P], F32)
        make_identity(nc, identity[:])
        sums = consts.tile([P, 2 * BLOCKS, P], F32)
        nc.vector.memset(sums[:], 0.0)
        warm = consts.tile([P, 1], F32)
        nc.scalar.copy(out=warm[:], in_=sums[:, 0, 0:1])
        ring = consts.tile([P, RING_ROWS, ROW], BF16)

        acc = [psum.tile([P, BLOCKS * P], F32, name="acc%d" % b) for b in range(2 * BLOCKS)]

        k_tiles = {}

        def copies(slot, rows, q, grouped, r0):
            for j in range(WORDS):
                copy = nc.vector.tensor_copy if j < PAIR else nc.scalar.copy
                regroup(copy, ring, slot, rows, q, j, grouped, r0)

        def quantise_k(chunk, q, pair, grouped):
            cols = PAIR * FREQS * K_ROWS
            codes = k_mx.tile([P, cols], U32, name="kc", tag="kc", align_bytes=64)
            scales = k_mx.tile([P, cols], U8, name="ks", tag="ks", align_bytes=64)
            quantise(nc, grouped, pair, codes, scales, cols)
            k_tiles[chunk, q, pair] = (codes, scales)

        def multiply(q, pair, grouped, rows):
            cols = PAIR * FREQS * rows
            codes = x_mx.tile([P, cols], U32, name="xc", tag="xc", align_bytes=64)
            scales = x_mx.tile([P, cols], U8, name="xs", tag="xs", align_bytes=64)
            quantise(nc, grouped, pair, codes, scales, cols)
            for i in range(PAIR):
                for s in range(2 * BLOCKS):
                    chunk, b = divmod(s, BLOCKS)
                    k_codes, k_scales = k_tiles[chunk, q, pair]
                    k0 = FREQS * K_ROWS * i + P * b
                    x0 = FREQS * rows * i + window_start(rows, b)
                    nc.tensor.matmul_mx(
                        out=acc[s][:, 0:WINDOW],
                        lhsT=k_codes[:, k0 : k0 + P].bitcast(FP8X4),
                        lhsT_scale=k_scales[:, k0 : k0 + P],
                        rhs=codes[:, x0 : x0 + WINDOW].bitcast(FP8X4),
                        rhs_scale=scales[:, x0 : x0 + WINDOW],
                        start=(q == 0 and pair == 0 and i == 0),
                        stop=(q == QUARTERS - 1 and pair == PAIRS - 1 and i == PAIR - 1),
                    )

        def empty(n0, rows):
            for s in range(2 * BLOCKS):
                b = s % BLOCKS
                copy = nc.vector.tensor_copy if s % 2 == 0 else nc.scalar.copy
                for e in range(BLOCK_FREQS):
                    first = rows * (BLOCK_FREQS * b + e) - window_start(rows, b)
                    part = slice(K_ROWS * e, K_ROWS * (e + 1))
                    copy(out=sums[part, s, n0 : n0 + rows], in_=acc[s][part, first : first + rows])

        sections = [(k_dct, K_ROWS * chunk, K_ROWS, chunk) for chunk in range(FILTERS // K_ROWS)]
        n0 = 0
        for rows in X_ROWS:
            sections.append((x_dct, n0, rows, None))
            n0 += rows

        late = []
        to_empty = []
        for index, (source, first, rows, chunk) in enumerate(sections):
            is_last = index == len(sections) - 1
            grouped = []
            r0 = 0
            for batch_rows in FIRST_LOADS if index == 0 else [rows]:
                slot = RING_ROWS - rows + r0
                load(nc, source, ring, slot, batch_rows, first + r0)
                for q in range(QUARTERS):
                    if q == len(grouped):
                        grouped.append(
                            groups.tile([P, WORDS, FREQS, rows, PACK], BF16, name="grouped", tag="grouped", align_bytes=64)
                        )
                    copies(slot, batch_rows, q, grouped[q], r0)
                    if r0 + batch_rows < rows:
                        continue
                    for work in late:
                        work()
                    if chunk is not None:
                        quantise_k(chunk, q, 0, grouped[q])
                        late = [lambda chunk=chunk, q=q, tile=grouped[q]: quantise_k(chunk, q, 1, tile)]
                    else:
                        if q == 0:
                            for done in to_empty:
                                empty(done[0], done[1])
                            to_empty = [(first, rows)]
                        multiply(q, 0, grouped[q], rows)
                        late = [lambda q=q, tile=grouped[q], rows=rows: multiply(q, 1, tile, rows)]
                    if is_last or q == QUARTERS - 1:
                        for work in late:
                            work()
                        late = []
                r0 += batch_rows
        for done in to_empty:
            empty(done[0], done[1])

        result = groups.tile([P, FILTERS, FREQS], F32, name="result", tag="grouped", align_bytes=64)
        flat_out = out.rearrange("n f y x -> n (f y x)")
        turn_copies = [nc.vector.tensor_copy, nc.scalar.copy]
        for chunk in range(2):
            turned = psum.tile([P, BLOCKS, P], F32, name="turned%d" % chunk, tag="acc%d" % chunk)
            for b in range(BLOCKS):
                nc.tensor.transpose(turned[:, b, :], sums[:, BLOCKS * chunk + b, :], identity[:])
            f0 = K_ROWS * chunk
            turn_copies[chunk](
                out=result[0:IMAGES, f0 : f0 + K_ROWS, :].rearrange("p f (b e) -> p f b e", e=BLOCK_FREQS),
                in_=turned[0:IMAGES].rearrange("p b (e f) -> p f b e", e=BLOCK_FREQS),
            )
            flat = result[:, f0 : f0 + K_ROWS, :].rearrange("p f w -> p (f w)")
            w0 = f0 * FREQS
            w1 = w0 + K_ROWS * FREQS
            nc.sync.dma_start(out=flat_out[0:STORE_CUT, w0:w1], in_=flat[0:STORE_CUT, :])
            nc.sync.dma_start(out=flat_out[STORE_CUT:IMAGES, w0:w1], in_=flat[STORE_CUT:IMAGES, :])
